import numpy as np
import ml_dtypes


def mxq(x, axis, fmt="e4m3"):
    dtype, down = {"e4m3": (ml_dtypes.float8_e4m3fn, 7), "e5m2": (ml_dtypes.float8_e5m2, 14)}[fmt]
    v = np.moveaxis(np.asarray(x, np.float32).astype(ml_dtypes.bfloat16).astype(np.float64), axis, -1)
    blocks = v.reshape(v.shape[:-1] + (-1, 32))
    amax = np.abs(blocks).max(-1, keepdims=True)
    byte = np.maximum(np.where(amax > 0, np.frexp(amax)[1] - 1 + 127, 0) - down, 1)
    scale = np.exp2(byte - 127.0)
    codes = (blocks / scale).astype(np.float32).astype(dtype).astype(np.float64)
    return np.moveaxis((codes * scale).reshape(v.shape), -1, axis)


WIDE = False


def mx_kscale(k):
    if not WIDE:
        return np.ones(k)
    levels = np.array([10, -10, 5, -5, 0])
    a = np.random.permutation(np.resize(levels, k // 512 * 4)).reshape(k // 512, 4)
    idx = np.arange(k)
    return np.exp2(a[idx // 512, idx % 128 // 32])


BF16 = ml_dtypes.bfloat16


def bf(x):
    return np.asarray(x, np.float32).astype(BF16)


def f64(x):
    return np.asarray(x).astype(np.float64)


M, K, N = 8192, 1024, 128


def softplus(v):
    return np.logaddexp(v, 0.0)


def setup_inputs():
    s = mx_kscale(K)
    w_std0 = np.log(np.expm1(0.5 / np.sqrt(K)))
    return {"x": bf(np.random.standard_normal((M, K)) * s),
            "w_loc": bf(np.random.standard_normal((K, N)) * 0.9 / np.sqrt(K) / s[:, None]),
            "w_std": bf(w_std0 + 0.3 * np.random.standard_normal((K, N))),
            "b_loc": bf(np.random.standard_normal((1, N)) * 0.5),
            "b_std": bf(-1.0 + 0.3 * np.random.standard_normal((1, N))),
            "eps_w": bf(np.random.standard_normal((K, N)) / s[:, None]),
            "eps_b": bf(np.random.standard_normal((1, N)))}


def reference(x, w_loc, w_std, b_loc, b_std, eps_w, eps_b):
    w = f64(w_loc) + softplus(f64(w_std)) * f64(eps_w)
    b = f64(b_loc) + softplus(f64(b_std)) * f64(eps_b)
    return (mxq(f64(x), 1, "e4m3") @ mxq(w, 0, "e4m3")) + b

@@ -1,0 +1,219 @@
+from contextlib import ExitStack
+
+import concourse.mybir as mybir
+from concourse.masks import make_identity
+
+F32 = mybir.dt.float32
+BF16 = mybir.dt.bfloat16
+U32 = mybir.dt.uint32
+U8 = mybir.dt.uint8
+FP8X4 = mybir.dt.float8_e4m3fn_x4
+ALU = mybir.AluOpType
+ACT = mybir.ActivationFunctionType
+
+P = 128
+ROWS, K, N = 8192, 1024, 128
+FLOPS = 2 * ROWS * K * N
+J = ROWS // P
+JC = 4
+NCH = J // JC
+CH = JC * K
+STORES = [(0, 32), (32, 48), (48, 56), (56, 60), (60, 64)]
+
+
+def dve_banks(c):
+    if c == 0:
+        return (0, 1)
+    if c == NCH - 1:
+        return (1, 3)
+    if c % 2 == 1:
+        return (0,)
+    return ()
+
+
+def tile_bayesiandenselayer_t_kernel(tc, x, w_loc, w_std, b_loc, b_std, eps_w, eps_b, out):
+    nc = tc.nc
+    with ExitStack() as ctx:
+        ctx.enter_context(tc.manual_schedule())
+        const = ctx.enter_context(tc.tile_pool(name="const", bufs=1))
+        xpool = ctx.enter_context(tc.tile_pool(name="xpool", bufs=1))
+        opool = ctx.enter_context(tc.tile_pool(name="opool", bufs=1))
+        gpool = ctx.enter_context(tc.tile_pool(name="gpool", bufs=3))
+        cpool = ctx.enter_context(tc.tile_pool(name="cpool", bufs=3))
+        tpsum = ctx.enter_context(tc.psum_pool(name="tpsum", bufs=6))
+        apsum = ctx.enter_context(tc.psum_pool(name="apsum", bufs=2))
+
+        xv = x.rearrange("(p j) k -> p (j k)", j=J)
+        ov = out.rearrange("(p j) n -> p (j n)", j=J)
+
+        zero_col = const.tile([P, 1], F32, name="zero_col")
+        one_col = const.tile([P, 1], F32, name="one_col")
+        warm = const.tile([P, 1], F32, name="warm")
+        brow = const.tile([P, 512], BF16, name="brow")
+        ones = const.tile([P, P], BF16, name="ones")
+        ident = const.tile([P, P], F32, name="ident")
+        nc.vector.memset(zero_col[:], 0.0)
+        nc.vector.memset(one_col[:], 1.0)
+        nc.vector.memset(brow[:], 0.0)
+        nc.vector.memset(ones[:], 1.0)
+        make_identity(nc, ident[:])
+        nc.scalar.activation(out=warm[:], in_=zero_col[:], func=ACT.Exp)
+
+        ws = const.tile([P, K], BF16, name="ws")
+        we = const.tile([P, K], BF16, name="we")
+        wl = const.tile([P, K], BF16, name="wl")
+
+        def load_w(dst, src):
+            nc.sync.dma_start(
+                out=dst[:].rearrange("p (b c) -> p b c", b=4),
+                in_=src.rearrange("(b p e) n -> p b (e n)", b=4, p=P, e=2),
+            )
+
+        x_sb = [xpool.tile([P, CH], BF16, name="x%d" % c) for c in range(NCH)]
+
+        def load_x(c):
+            nc.sync.dma_start(out=x_sb[c][:], in_=xv[:, c * CH : (c + 1) * CH])
+
+        nc.scalar.dma_start(out=brow[0:1, 0:N], in_=b_loc)
+        nc.scalar.dma_start(out=brow[0:1, N : 2 * N], in_=b_std)
+        nc.scalar.dma_start(out=brow[0:1, 2 * N : 3 * N], in_=eps_b)
+        load_w(ws, w_std)
+        load_x(0)
+        load_w(we, eps_w)
+        load_w(wl, w_loc)
+        for c in range(1, NCH):
+            load_x(c)
+
+        banks = {}
+        grouped = {}
+        codes = {}
+        scales = {}
+        accs = {}
+        otiles = {}
+
+        def transposes(c):
+            xw = x_sb[c][:].bitcast(F32)
+            for jj in range(JC):
+                bank = tpsum.tile([P, 512], F32, name="xt")
+                for b in range(4):
+                    col = jj * 512 + b * P
+                    nc.tensor.transpose(bank[:, b * P : (b + 1) * P], xw[:, col : col + P], ident[:])
+                banks[(c, jj)] = bank
+
+        def evacuate(c):
+            g_t = gpool.tile([P, CH], BF16, name="grouped", align_bytes=64)
+            grouped[c] = g_t
+            gw = g_t[:].bitcast(F32)
+            on_dve = dve_banks(c)
+            for jj in range(JC):
+                dst = gw[:, jj * 512 : (jj + 1) * 512].rearrange("p (g r u) -> p g r u", g=2, r=P, u=2)
+                src = banks[(c, jj)][:].rearrange("p (g u r) -> p g r u", g=2, u=2, r=P)
+                if jj in on_dve:
+                    nc.vector.tensor_copy(out=dst, in_=src)
+                else:
+                    nc.scalar.copy(out=dst, in_=src)
+
+        def quantise(c):
+            c_t = cpool.tile([P, CH // 4], U32, name="codes", align_bytes=64)
+            s_t = cpool.tile([P, CH // 4], U8, name="scales", align_bytes=64)
+            codes[c] = c_t
+            scales[c] = s_t
+            for h in range(2):
+                nc.vector.quantize_mx(
+                    out=c_t[:, h * 512 : (h + 1) * 512].bitcast(FP8X4),
+                    scales=s_t[:, h * 512 : (h + 1) * 512],
+                    in_=grouped[c][:, h * 2048 : (h + 1) * 2048],
+                )
+
+        def multiply(c):
+            acc = apsum.tile([P, 512], F32, name="acc")
+            accs[c] = acc
+            for jj in range(JC):
+                for g in range(2):
+                    col = (jj * 2 + g) * P
+                    nc.tensor.matmul_mx(
+                        out=acc[:, jj * N : (jj + 1) * N],
+                        lhsT=codes[c][:, col : col + P].bitcast(FP8X4),
+                        lhsT_scale=scales[c][:, col : col + P],
+                        rhs=wcodes[:, g * N : (g + 1) * N].bitcast(FP8X4),
+                        rhs_scale=wscales[:, g * N : (g + 1) * N],
+                        start=(g == 0),
+                        stop=(g == 1),
+                    )
+
+        def finish(c):
+            j0 = c * JC
+            for (a, b) in STORES:
+                if a <= j0 < b:
+                    if a == j0:
+                        otiles[a] = opool.tile([P, (b - a) * N], F32, name="o%d" % a)
+                    o_t = otiles[a]
+                    off = (j0 - a) * N
+                    nc.vector.tensor_tensor(
+                        out=o_t[:, off : off + JC * N].rearrange("p (j n) -> p j n", j=JC),
+                        in0=accs[c][:].rearrange("p (j n) -> p j n", j=JC),
+                        in1=bias[:].unsqueeze(1).to_broadcast([P, JC, N]),
+                        op=ALU.add,
+                    )
+                    if j0 + JC == b:
+                        nc.sync.dma_start(out=ov[:, a * N : b * N], in_=o_t[:])
+
+        na = const.tile([P, K], BF16, name="na")
+        ex = const.tile([P, K], F32, name="ex")
+        sp = const.tile([P, K], F32, name="sp")
+        wg = const.tile([P, K], BF16, name="wg", align_bytes=64)
+        wcodes = const.tile([P, K // 4], U32, name="wcodes", align_bytes=64)
+        wscales = const.tile([P, K // 4], U8, name="wscales", align_bytes=64)
+        bsb = const.tile([P, 3 * N], F32, name="bsb")
+        nb = const.tile([P, N], F32, name="nb")
+        eb = const.tile([P, N], F32, name="eb")
+        bias = const.tile([P, N], F32, name="bias")
+        H = K // 2
+
+        bps = apsum.tile([P, 512], F32, name="acc")
+        nc.tensor.matmul(out=bps[:], lhsT=ones[:], rhs=brow[:], start=True, stop=True)
+
+        for g in range(2):
+            s = slice(g * H, (g + 1) * H)
+            nc.vector.scalar_tensor_tensor(out=na[:, s], in0=ws[:, s], scalar=-1.0, in1=ws[:, s], op0=ALU.mult, op1=ALU.min)
+            nc.scalar.activation(out=ex[:, s], in_=na[:, s], func=ACT.Exp)
+        nc.vector.tensor_copy(out=bsb[:], in_=bps[:, 0 : 3 * N])
+        b_l = bsb[:, 0:N]
+        b_s = bsb[:, N : 2 * N]
+        b_e = bsb[:, 2 * N : 3 * N]
+        nc.vector.scalar_tensor_tensor(out=nb[:], in0=b_s, scalar=-1.0, in1=b_s, op0=ALU.mult, op1=ALU.min)
+        nc.scalar.activation(out=eb[:], in_=nb[:], func=ACT.Exp)
+        for g in range(2):
+            s = slice(g * H, (g + 1) * H)
+            nc.scalar.activation(out=ex[:, s], in_=ex[:, s], func=ACT.Ln, bias=one_col[:], scale=1.0)
+        nc.scalar.activation(out=eb[:], in_=eb[:], func=ACT.Ln, bias=one_col[:], scale=1.0)
+
+        transposes(0)
+        evacuate(0)
+
+        for g in range(2):
+            s = slice(g * H, (g + 1) * H)
+            nc.vector.scalar_tensor_tensor(out=sp[:, s], in0=ws[:, s], scalar=0.0, in1=ex[:, s], op0=ALU.max, op1=ALU.add)
+            nc.vector.tensor_tensor(out=sp[:, s], in0=sp[:, s], in1=we[:, s], op=ALU.mult)
+            nc.vector.tensor_tensor(
+                out=wg[:, s].rearrange("p (n t) -> p n t", n=N, t=4),
+                in0=sp[:, s].rearrange("p (t n) -> p n t", n=N, t=4),
+                in1=wl[:, s].rearrange("p (t n) -> p n t", n=N, t=4),
+                op=ALU.add,
+            )
+        nc.vector.scalar_tensor_tensor(out=nb[:], in0=b_s, scalar=0.0, in1=eb[:], op0=ALU.max, op1=ALU.add)
+        nc.vector.quantize_mx(out=wcodes[:].bitcast(FP8X4), scales=wscales[:], in_=wg[:])
+        nc.vector.tensor_tensor(out=nb[:], in0=nb[:], in1=b_e, op=ALU.mult)
+        nc.vector.tensor_tensor(out=bias[:], in0=nb[:], in1=b_l, op=ALU.add)
+
+        quantise(0)
+        for c in range(1, NCH):
+            transposes(c)
+            multiply(c - 1)
+            evacuate(c)
+            if c >= 2:
+                finish(c - 2)
+            quantise(c)
+        multiply(NCH - 1)
+        finish(NCH - 2)
+        finish(NCH - 1)

@@ -19,6 +19,7 @@ JC = 4
 NCH = J // JC
 CH = JC * K
 STORES = [(0, 32), (32, 48), (48, 56), (56, 60), (60, 64)]
+CLAMP = 30.0
 
 
 def dve_banks(c):
@@ -26,7 +27,7 @@ def dve_banks(c):
         return (0, 1)
     if c == NCH - 1:
         return (1, 3)
-    if c % 2 == 1:
+    if c % 4 == 2:
         return (0,)
     return ()
 
@@ -39,7 +40,7 @@ def tile_bayesiandenselayer_t_kernel(tc, x, w_loc, w_std, b_loc, b_std, eps_w, e
         xpool = ctx.enter_context(tc.tile_pool(name="xpool", bufs=1))
         opool = ctx.enter_context(tc.tile_pool(name="opool", bufs=1))
         gpool = ctx.enter_context(tc.tile_pool(name="gpool", bufs=3))
-        cpool = ctx.enter_context(tc.tile_pool(name="cpool", bufs=3))
+        cpool = ctx.enter_context(tc.tile_pool(name="cpool", bufs=4))
         tpsum = ctx.enter_context(tc.psum_pool(name="tpsum", bufs=6))
         apsum = ctx.enter_context(tc.psum_pool(name="apsum", bufs=2))
 
@@ -52,11 +53,14 @@ def tile_bayesiandenselayer_t_kernel(tc, x, w_loc, w_std, b_loc, b_std, eps_w, e
         brow = const.tile([P, 512], BF16, name="brow")
         ones = const.tile([P, P], BF16, name="ones")
         ident = const.tile([P, P], F32, name="ident")
+        nc.vector.memset(brow[:], 0.0)
         nc.vector.memset(zero_col[:], 0.0)
         nc.vector.memset(one_col[:], 1.0)
-        nc.vector.memset(brow[:], 0.0)
         nc.vector.memset(ones[:], 1.0)
         make_identity(nc, ident[:])
+        nc.scalar.dma_start(out=brow[0:1, N : 2 * N], in_=b_std)
+        nc.scalar.dma_start(out=brow[0:1, 0:N], in_=b_loc)
+        nc.scalar.dma_start(out=brow[0:1, 2 * N : 3 * N], in_=eps_b)
         nc.scalar.activation(out=warm[:], in_=zero_col[:], func=ACT.Exp)
 
         ws = const.tile([P, K], BF16, name="ws")
@@ -74,9 +78,6 @@ def tile_bayesiandenselayer_t_kernel(tc, x, w_loc, w_std, b_loc, b_std, eps_w, e
         def load_x(c):
             nc.sync.dma_start(out=x_sb[c][:], in_=xv[:, c * CH : (c + 1) * CH])
 
-        nc.scalar.dma_start(out=brow[0:1, 0:N], in_=b_loc)
-        nc.scalar.dma_start(out=brow[0:1, N : 2 * N], in_=b_std)
-        nc.scalar.dma_start(out=brow[0:1, 2 * N : 3 * N], in_=eps_b)
         load_w(ws, w_std)
         load_x(0)
         load_w(we, eps_w)
@@ -160,7 +161,6 @@ def tile_bayesiandenselayer_t_kernel(tc, x, w_loc, w_std, b_loc, b_std, eps_w, e
 
         na = const.tile([P, K], BF16, name="na")
         ex = const.tile([P, K], F32, name="ex")
-        sp = const.tile([P, K], F32, name="sp")
         wg = const.tile([P, K], BF16, name="wg", align_bytes=64)
         wcodes = const.tile([P, K // 4], U32, name="wcodes", align_bytes=64)
         wscales = const.tile([P, K // 4], U8, name="wscales", align_bytes=64)
@@ -173,15 +173,13 @@ def tile_bayesiandenselayer_t_kernel(tc, x, w_loc, w_std, b_loc, b_std, eps_w, e
         bps = apsum.tile([P, 512], F32, name="acc")
         nc.tensor.matmul(out=bps[:], lhsT=ones[:], rhs=brow[:], start=True, stop=True)
 
-        for g in range(2):
-            s = slice(g * H, (g + 1) * H)
-            nc.vector.scalar_tensor_tensor(out=na[:, s], in0=ws[:, s], scalar=-1.0, in1=ws[:, s], op0=ALU.mult, op1=ALU.min)
-            nc.scalar.activation(out=ex[:, s], in_=na[:, s], func=ACT.Exp)
+        nc.vector.tensor_scalar_min(out=na[:], in0=ws[:], scalar1=CLAMP)
+        nc.scalar.activation(out=ex[:], in_=na[:], func=ACT.Exp)
         nc.vector.tensor_copy(out=bsb[:], in_=bps[:, 0 : 3 * N])
         b_l = bsb[:, 0:N]
         b_s = bsb[:, N : 2 * N]
         b_e = bsb[:, 2 * N : 3 * N]
-        nc.vector.scalar_tensor_tensor(out=nb[:], in0=b_s, scalar=-1.0, in1=b_s, op0=ALU.mult, op1=ALU.min)
+        nc.vector.tensor_scalar_min(out=nb[:], in0=b_s, scalar1=CLAMP)
         nc.scalar.activation(out=eb[:], in_=nb[:], func=ACT.Exp)
         for g in range(2):
             s = slice(g * H, (g + 1) * H)
@@ -193,15 +191,15 @@ def tile_bayesiandenselayer_t_kernel(tc, x, w_loc, w_std, b_loc, b_std, eps_w, e
 
         for g in range(2):
             s = slice(g * H, (g + 1) * H)
-            nc.vector.scalar_tensor_tensor(out=sp[:, s], in0=ws[:, s], scalar=0.0, in1=ex[:, s], op0=ALU.max, op1=ALU.add)
-            nc.vector.tensor_tensor(out=sp[:, s], in0=sp[:, s], in1=we[:, s], op=ALU.mult)
+            nc.vector.tensor_tensor(out=ex[:, s], in0=ex[:, s], in1=ws[:, s], op=ALU.max)
+            nc.vector.tensor_tensor(out=ex[:, s], in0=ex[:, s], in1=we[:, s], op=ALU.mult)
             nc.vector.tensor_tensor(
                 out=wg[:, s].rearrange("p (n t) -> p n t", n=N, t=4),
-                in0=sp[:, s].rearrange("p (t n) -> p n t", n=N, t=4),
+                in0=ex[:, s].rearrange("p (t n) -> p n t", n=N, t=4),
                 in1=wl[:, s].rearrange("p (t n) -> p n t", n=N, t=4),
                 op=ALU.add,
             )
-        nc.vector.scalar_tensor_tensor(out=nb[:], in0=b_s, scalar=0.0, in1=eb[:], op0=ALU.max, op1=ALU.add)
+        nc.vector.tensor_tensor(out=nb[:], in0=eb[:], in1=b_s, op=ALU.max)
         nc.vector.quantize_mx(out=wcodes[:].bitcast(FP8X4), scales=wscales[:], in_=wg[:])
         nc.vector.tensor_tensor(out=nb[:], in0=nb[:], in1=b_e, op=ALU.mult)
         nc.vector.tensor_tensor(out=bias[:], in0=nb[:], in1=b_l, op=ALU.add)
@@ -209,11 +207,14 @@ def tile_bayesiandenselayer_t_kernel(tc, x, w_loc, w_std, b_loc, b_std, eps_w, e
         quantise(0)
         for c in range(1, NCH):
             transposes(c)
-            multiply(c - 1)
-            evacuate(c)
             if c >= 2:
-                finish(c - 2)
+                multiply(c - 2)
+            evacuate(c)
+            if c >= 3:
+                finish(c - 3)
             quantise(c)
+        multiply(NCH - 2)
+        finish(NCH - 3)
         multiply(NCH - 1)
         finish(NCH - 2)
         finish(NCH - 1)

@@ -18,7 +18,7 @@ J = ROWS // P
 JC = 4
 NCH = J // JC
 CH = JC * K
-STORES = [(0, 32), (32, 48), (48, 56), (56, 60), (60, 64)]
+STORES = [(4 * i, 4 * i + 4) for i in range(16)]
 CLAMP = 30.0
 
 
@@ -44,8 +44,8 @@ def tile_bayesiandenselayer_t_kernel(tc, x, w_loc, w_std, b_loc, b_std, eps_w, e
         tpsum = ctx.enter_context(tc.psum_pool(name="tpsum", bufs=6))
         apsum = ctx.enter_context(tc.psum_pool(name="apsum", bufs=2))
 
-        xv = x.rearrange("(p j) k -> p (j k)", j=J)
-        ov = out.rearrange("(p j) n -> p (j n)", j=J)
+        xv = x.rearrange("(c p t) k -> c p (t k)", c=NCH, p=P, t=JC)
+        ov = out.rearrange("(c p t) n -> c p (t n)", c=NCH, p=P, t=JC)
 
         zero_col = const.tile([P, 1], F32, name="zero_col")
         one_col = const.tile([P, 1], F32, name="one_col")
@@ -76,7 +76,7 @@ def tile_bayesiandenselayer_t_kernel(tc, x, w_loc, w_std, b_loc, b_std, eps_w, e
         x_sb = [xpool.tile([P, CH], BF16, name="x%d" % c) for c in range(NCH)]
 
         def load_x(c):
-            nc.sync.dma_start(out=x_sb[c][:], in_=xv[:, c * CH : (c + 1) * CH])
+            nc.sync.dma_start(out=x_sb[c][:], in_=xv[c])
 
         load_w(ws, w_std)
         load_x(0)
@@ -157,7 +157,7 @@ def tile_bayesiandenselayer_t_kernel(tc, x, w_loc, w_std, b_loc, b_std, eps_w, e
                         op=ALU.add,
                     )
                     if j0 + JC == b:
-                        nc.sync.dma_start(out=ov[:, a * N : b * N], in_=o_t[:])
+                        nc.sync.dma_start(out=ov[c], in_=o_t[:])
 
         na = const.tile([P, K], BF16, name="na")
         ex = const.tile([P, K], F32, name="ex")

@@ -18,16 +18,16 @@ J = ROWS // P
 JC = 4
 NCH = J // JC
 CH = JC * K
-STORES = [(4 * i, 4 * i + 4) for i in range(16)]
+STORES = [(0, 32), (32, 48), (48, 56), (56, 60), (60, 62), (62, 64)]
 CLAMP = 30.0
+M_LAG = 3
+O_LAG = 4
 
 
 def dve_banks(c):
     if c == 0:
-        return (0, 1)
-    if c == NCH - 1:
-        return (1, 3)
-    if c % 4 == 2:
+        return (0, 1, 2)
+    if 4 <= c < NCH - 1 and c % 2 == 0:
         return (0,)
     return ()
 
@@ -44,8 +44,8 @@ def tile_bayesiandenselayer_t_kernel(tc, x, w_loc, w_std, b_loc, b_std, eps_w, e
         tpsum = ctx.enter_context(tc.psum_pool(name="tpsum", bufs=6))
         apsum = ctx.enter_context(tc.psum_pool(name="apsum", bufs=2))
 
-        xv = x.rearrange("(c p t) k -> c p (t k)", c=NCH, p=P, t=JC)
-        ov = out.rearrange("(c p t) n -> c p (t n)", c=NCH, p=P, t=JC)
+        xv = x.rearrange("(p j) k -> p (j k)", j=J)
+        ov = out.rearrange("(p j) n -> p (j n)", j=J)
 
         zero_col = const.tile([P, 1], F32, name="zero_col")
         one_col = const.tile([P, 1], F32, name="one_col")
@@ -75,15 +75,13 @@ def tile_bayesiandenselayer_t_kernel(tc, x, w_loc, w_std, b_loc, b_std, eps_w, e
 
         x_sb = [xpool.tile([P, CH], BF16, name="x%d" % c) for c in range(NCH)]
 
-        def load_x(c):
-            nc.sync.dma_start(out=x_sb[c][:], in_=xv[c])
-
         load_w(ws, w_std)
-        load_x(0)
+        nc.sync.dma_start(out=x_sb[0][:, 0 : CH // 2], in_=xv[:, 0 : CH // 2])
+        nc.sync.dma_start(out=x_sb[0][:, CH // 2 : CH], in_=xv[:, CH // 2 : CH])
         load_w(we, eps_w)
         load_w(wl, w_loc)
         for c in range(1, NCH):
-            load_x(c)
+            nc.sync.dma_start(out=x_sb[c][:], in_=xv[:, c * CH : (c + 1) * CH])
 
         banks = {}
         grouped = {}
@@ -114,26 +112,25 @@ def tile_bayesiandenselayer_t_kernel(tc, x, w_loc, w_std, b_loc, b_std, eps_w, e
                 else:
                     nc.scalar.copy(out=dst, in_=src)
 
-        def quantise(c):
-            c_t = cpool.tile([P, CH // 4], U32, name="codes", align_bytes=64)
-            s_t = cpool.tile([P, CH // 4], U8, name="scales", align_bytes=64)
-            codes[c] = c_t
-            scales[c] = s_t
-            for h in range(2):
-                nc.vector.quantize_mx(
-                    out=c_t[:, h * 512 : (h + 1) * 512].bitcast(FP8X4),
-                    scales=s_t[:, h * 512 : (h + 1) * 512],
-                    in_=grouped[c][:, h * 2048 : (h + 1) * 2048],
-                )
+        def quantise(c, part, parts):
+            if part == 0:
+                codes[c] = cpool.tile([P, CH // 4], U32, name="codes", align_bytes=64)
+                scales[c] = cpool.tile([P, CH // 4], U8, name="scales", align_bytes=64)
+            wd = CH // 4 // parts
+            nc.vector.quantize_mx(
+                out=codes[c][:, part * wd : (part + 1) * wd].bitcast(FP8X4),
+                scales=scales[c][:, part * wd : (part + 1) * wd],
+                in_=grouped[c][:, part * 4 * wd : (part + 1) * 4 * wd],
+            )
 
-        def multiply(c):
-            acc = apsum.tile([P, 512], F32, name="acc")
-            accs[c] = acc
-            for jj in range(JC):
+        def multiply(c, first, count, pool, name):
+            acc = pool.tile([P, 512], F32, name=name)
+            accs[(c, first)] = acc
+            for i in range(count):
                 for g in range(2):
-                    col = (jj * 2 + g) * P
+                    col = ((first + i) * 2 + g) * P
                     nc.tensor.matmul_mx(
-                        out=acc[:, jj * N : (jj + 1) * N],
+                        out=acc[:, i * N : (i + 1) * N],
                         lhsT=codes[c][:, col : col + P].bitcast(FP8X4),
                         lhsT_scale=scales[c][:, col : col + P],
                         rhs=wcodes[:, g * N : (g + 1) * N].bitcast(FP8X4),
@@ -142,8 +139,8 @@ def tile_bayesiandenselayer_t_kernel(tc, x, w_loc, w_std, b_loc, b_std, eps_w, e
                         stop=(g == 1),
                     )
 
-        def finish(c):
-            j0 = c * JC
+        def finish(c, first, count):
+            j0 = c * JC + first
             for (a, b) in STORES:
                 if a <= j0 < b:
                     if a == j0:
@@ -151,70 +148,78 @@ def tile_bayesiandenselayer_t_kernel(tc, x, w_loc, w_std, b_loc, b_std, eps_w, e
                     o_t = otiles[a]
                     off = (j0 - a) * N
                     nc.vector.tensor_tensor(
-                        out=o_t[:, off : off + JC * N].rearrange("p (j n) -> p j n", j=JC),
-                        in0=accs[c][:].rearrange("p (j n) -> p j n", j=JC),
-                        in1=bias[:].unsqueeze(1).to_broadcast([P, JC, N]),
+                        out=o_t[:, off : off + count * N].rearrange("p (j n) -> p j n", j=count),
+                        in0=accs[(c, first)][:, 0 : count * N].rearrange("p (j n) -> p j n", j=count),
+                        in1=bias[:].unsqueeze(1).to_broadcast([P, count, N]),
                         op=ALU.add,
                     )
-                    if j0 + JC == b:
-                        nc.sync.dma_start(out=ov[c], in_=o_t[:])
+                    if j0 + count == b:
+                        nc.sync.dma_start(out=ov[:, a * N : b * N], in_=o_t[:])
 
         na = const.tile([P, K], BF16, name="na")
-        ex = const.tile([P, K], F32, name="ex")
+        ex = const.tile([P, K + N], F32, name="ex")
         wg = const.tile([P, K], BF16, name="wg", align_bytes=64)
         wcodes = const.tile([P, K // 4], U32, name="wcodes", align_bytes=64)
         wscales = const.tile([P, K // 4], U8, name="wscales", align_bytes=64)
         bsb = const.tile([P, 3 * N], F32, name="bsb")
         nb = const.tile([P, N], F32, name="nb")
-        eb = const.tile([P, N], F32, name="eb")
         bias = const.tile([P, N], F32, name="bias")
         H = K // 2
+        eb = ex[:, K : K + N]
 
         bps = apsum.tile([P, 512], F32, name="acc")
         nc.tensor.matmul(out=bps[:], lhsT=ones[:], rhs=brow[:], start=True, stop=True)
 
         nc.vector.tensor_scalar_min(out=na[:], in0=ws[:], scalar1=CLAMP)
-        nc.scalar.activation(out=ex[:], in_=na[:], func=ACT.Exp)
+        nc.scalar.activation(out=ex[:, 0:K], in_=na[:], func=ACT.Exp)
         nc.vector.tensor_copy(out=bsb[:], in_=bps[:, 0 : 3 * N])
         b_l = bsb[:, 0:N]
         b_s = bsb[:, N : 2 * N]
         b_e = bsb[:, 2 * N : 3 * N]
         nc.vector.tensor_scalar_min(out=nb[:], in0=b_s, scalar1=CLAMP)
-        nc.scalar.activation(out=eb[:], in_=nb[:], func=ACT.Exp)
-        for g in range(2):
-            s = slice(g * H, (g + 1) * H)
-            nc.scalar.activation(out=ex[:, s], in_=ex[:, s], func=ACT.Ln, bias=one_col[:], scale=1.0)
-        nc.scalar.activation(out=eb[:], in_=eb[:], func=ACT.Ln, bias=one_col[:], scale=1.0)
+        nc.scalar.activation(out=eb, in_=nb[:], func=ACT.Exp)
+        nc.scalar.activation(out=ex[:, 0:H], in_=ex[:, 0:H], func=ACT.Ln, bias=one_col[:], scale=1.0)
+        nc.scalar.activation(out=ex[:, H : K + N], in_=ex[:, H : K + N], func=ACT.Ln, bias=one_col[:], scale=1.0)
 
-        transposes(0)
-        evacuate(0)
+        def sample_w():
+            for g in range(2):
+                s = slice(g * H, (g + 1) * H)
+                nc.vector.tensor_tensor(out=ex[:, s], in0=ex[:, s], in1=ws[:, s], op=ALU.max)
+                nc.vector.tensor_tensor(out=ex[:, s], in0=ex[:, s], in1=we[:, s], op=ALU.mult)
+                nc.vector.tensor_tensor(
+                    out=wg[:, s].rearrange("p (n t) -> p n t", n=N, t=4),
+                    in0=ex[:, s].rearrange("p (t n) -> p n t", n=N, t=4),
+                    in1=wl[:, s].rearrange("p (t n) -> p n t", n=N, t=4),
+                    op=ALU.add,
+                )
 
-        for g in range(2):
-            s = slice(g * H, (g + 1) * H)
-            nc.vector.tensor_tensor(out=ex[:, s], in0=ex[:, s], in1=ws[:, s], op=ALU.max)
-            nc.vector.tensor_tensor(out=ex[:, s], in0=ex[:, s], in1=we[:, s], op=ALU.mult)
-            nc.vector.tensor_tensor(
-                out=wg[:, s].rearrange("p (n t) -> p n t", n=N, t=4),
-                in0=ex[:, s].rearrange("p (t n) -> p n t", n=N, t=4),
-                in1=wl[:, s].rearrange("p (t n) -> p n t", n=N, t=4),
-                op=ALU.add,
-            )
-        nc.vector.tensor_tensor(out=nb[:], in0=eb[:], in1=b_s, op=ALU.max)
-        nc.vector.quantize_mx(out=wcodes[:].bitcast(FP8X4), scales=wscales[:], in_=wg[:])
-        nc.vector.tensor_tensor(out=nb[:], in0=nb[:], in1=b_e, op=ALU.mult)
-        nc.vector.tensor_tensor(out=bias[:], in0=nb[:], in1=b_l, op=ALU.add)
+        def sample_b():
+            nc.vector.tensor_tensor(out=nb[:], in0=eb, in1=b_s, op=ALU.max)
+            nc.vector.tensor_tensor(out=nb[:], in0=nb[:], in1=b_e, op=ALU.mult)
+            nc.vector.tensor_tensor(out=bias[:], in0=nb[:], in1=b_l, op=ALU.add)
 
-        quantise(0)
-        for c in range(1, NCH):
+        for c in range(NCH):
             transposes(c)
-            if c >= 2:
-                multiply(c - 2)
+            if c >= M_LAG:
+                multiply(c - M_LAG, 0, JC, apsum, "acc")
             evacuate(c)
-            if c >= 3:
-                finish(c - 3)
-            quantise(c)
-        multiply(NCH - 2)
-        finish(NCH - 3)
-        multiply(NCH - 1)
-        finish(NCH - 2)
-        finish(NCH - 1)
+            if c >= O_LAG:
+                finish(c - O_LAG, 0, JC)
+            if c == 1:
+                sample_w()
+                sample_b()
+                nc.vector.quantize_mx(out=wcodes[:].bitcast(FP8X4), scales=wscales[:], in_=wg[:])
+            if c >= 1:
+                quantise(c - 1, 0, 1)
+        L = NCH - 1
+        multiply(L - 2, 0, JC, apsum, "acc")
+        finish(L - 3, 0, JC)
+        quantise(L, 0, 2)
+        quantise(L, 1, 2)
+        multiply(L - 1, 0, JC, apsum, "acc")
+        finish(L - 2, 0, JC)
+        multiply(L, 0, 2, tpsum, "xt")
+        multiply(L, 2, 2, tpsum, "xt")
+        finish(L - 1, 0, JC)
+        finish(L, 0, 2)
+        finish(L, 2, 2)

@@ -27,7 +27,7 @@ O_LAG = 4
 def dve_banks(c):
     if c == 0:
         return (0, 1, 2)
-    if 4 <= c < NCH - 1 and c % 2 == 0:
+    if 3 <= c <= 13 and c % 4 != 2:
         return (0,)
     return ()
 

@@ -27,7 +27,7 @@ O_LAG = 4
 def dve_banks(c):
     if c == 0:
         return (0, 1, 2)
-    if 3 <= c <= 13 and c % 4 != 2:
+    if c in (6, 11):
         return (0,)
     return ()
 
@@ -164,7 +164,6 @@ def tile_bayesiandenselayer_t_kernel(tc, x, w_loc, w_std, b_loc, b_std, eps_w, e
         bsb = const.tile([P, 3 * N], F32, name="bsb")
         nb = const.tile([P, N], F32, name="nb")
         bias = const.tile([P, N], F32, name="bias")
-        H = K // 2
         eb = ex[:, K : K + N]
 
         bps = apsum.tile([P, 512], F32, name="acc")
@@ -178,20 +177,17 @@ def tile_bayesiandenselayer_t_kernel(tc, x, w_loc, w_std, b_loc, b_std, eps_w, e
         b_e = bsb[:, 2 * N : 3 * N]
         nc.vector.tensor_scalar_min(out=nb[:], in0=b_s, scalar1=CLAMP)
         nc.scalar.activation(out=eb, in_=nb[:], func=ACT.Exp)
-        nc.scalar.activation(out=ex[:, 0:H], in_=ex[:, 0:H], func=ACT.Ln, bias=one_col[:], scale=1.0)
-        nc.scalar.activation(out=ex[:, H : K + N], in_=ex[:, H : K + N], func=ACT.Ln, bias=one_col[:], scale=1.0)
+        nc.scalar.activation(out=ex[:], in_=ex[:], func=ACT.Ln, bias=one_col[:], scale=1.0)
 
         def sample_w():
-            for g in range(2):
-                s = slice(g * H, (g + 1) * H)
-                nc.vector.tensor_tensor(out=ex[:, s], in0=ex[:, s], in1=ws[:, s], op=ALU.max)
-                nc.vector.tensor_tensor(out=ex[:, s], in0=ex[:, s], in1=we[:, s], op=ALU.mult)
-                nc.vector.tensor_tensor(
-                    out=wg[:, s].rearrange("p (n t) -> p n t", n=N, t=4),
-                    in0=ex[:, s].rearrange("p (t n) -> p n t", n=N, t=4),
-                    in1=wl[:, s].rearrange("p (t n) -> p n t", n=N, t=4),
-                    op=ALU.add,
-                )
+            nc.vector.tensor_tensor(out=ex[:, 0:K], in0=ex[:, 0:K], in1=ws[:], op=ALU.max)
+            nc.vector.tensor_tensor(out=ex[:, 0:K], in0=ex[:, 0:K], in1=we[:], op=ALU.mult)
+            nc.vector.tensor_tensor(
+                out=wg[:].rearrange("p (g n t) -> p g n t", g=2, n=N, t=4),
+                in0=ex[:, 0:K].rearrange("p (g t n) -> p g n t", g=2, n=N, t=4),
+                in1=wl[:].rearrange("p (g t n) -> p g n t", g=2, n=N, t=4),
+                op=ALU.add,
+            )
 
         def sample_b():
             nc.vector.tensor_tensor(out=nb[:], in0=eb, in1=b_s, op=ALU.max)

@@ -90,9 +90,9 @@ def tile_bayesiandenselayer_t_kernel(tc, x, w_loc, w_std, b_loc, b_std, eps_w, e
         accs = {}
         otiles = {}
 
-        def transposes(c):
+        def transposes(c, first, count):
             xw = x_sb[c][:].bitcast(F32)
-            for jj in range(JC):
+            for jj in range(first, first + count):
                 bank = tpsum.tile([P, 512], F32, name="xt")
                 for b in range(4):
                     col = jj * 512 + b * P
@@ -122,6 +122,24 @@ def tile_bayesiandenselayer_t_kernel(tc, x, w_loc, w_std, b_loc, b_std, eps_w, e
                 scales=scales[c][:, part * wd : (part + 1) * wd],
                 in_=grouped[c][:, part * 4 * wd : (part + 1) * 4 * wd],
             )
+
+        def multiply_part(c, first, count):
+            if first == 0:
+                acc0 = apsum.tile([P, 512], F32, name="acc")
+                accs[(c, 0)] = acc0
+            acc = accs[(c, 0)]
+            for i in range(first, first + count):
+                for g in range(2):
+                    col = (i * 2 + g) * P
+                    nc.tensor.matmul_mx(
+                        out=acc[:, i * N : (i + 1) * N],
+                        lhsT=codes[c][:, col : col + P].bitcast(FP8X4),
+                        lhsT_scale=scales[c][:, col : col + P],
+                        rhs=wcodes[:, g * N : (g + 1) * N].bitcast(FP8X4),
+                        rhs_scale=wscales[:, g * N : (g + 1) * N],
+                        start=(g == 0),
+                        stop=(g == 1),
+                    )
 
         def multiply(c, first, count, pool, name):
             acc = pool.tile([P, 512], F32, name=name)
@@ -195,9 +213,12 @@ def tile_bayesiandenselayer_t_kernel(tc, x, w_loc, w_std, b_loc, b_std, eps_w, e
             nc.vector.tensor_tensor(out=bias[:], in0=nb[:], in1=b_l, op=ALU.add)
 
         for c in range(NCH):
-            transposes(c)
+            transposes(c, 0, 2)
             if c >= M_LAG:
-                multiply(c - M_LAG, 0, JC, apsum, "acc")
+                multiply_part(c - M_LAG, 0, 2)
+            transposes(c, 2, 2)
+            if c >= M_LAG:
+                multiply_part(c - M_LAG, 2, 2)
             evacuate(c)
             if c >= O_LAG:
                 finish(c - O_LAG, 0, JC)

from contextlib import ExitStack

import concourse.mybir as mybir
from concourse.masks import make_identity

F32 = mybir.dt.float32
BF16 = mybir.dt.bfloat16
U32 = mybir.dt.uint32
U8 = mybir.dt.uint8
FP8X4 = mybir.dt.float8_e4m3fn_x4
ALU = mybir.AluOpType
ACT = mybir.ActivationFunctionType

P = 128
ROWS, K, N = 8192, 1024, 128
FLOPS = 2 * ROWS * K * N
J = ROWS // P
JC = 4
NCH = J // JC
CH = JC * K
STORES = [(0, 32), (32, 48), (48, 56), (56, 60), (60, 62), (62, 64)]
CLAMP = 30.0
M_LAG = 3
O_LAG = 4


def dve_banks(c):
    if c == 0:
        return (0, 1, 2)
    if c in (6, 11):
        return (0,)
    return ()


def tile_bayesiandenselayer_t_kernel(tc, x, w_loc, w_std, b_loc, b_std, eps_w, eps_b, out):
    nc = tc.nc
    with ExitStack() as ctx:
        ctx.enter_context(tc.manual_schedule())
        const = ctx.enter_context(tc.tile_pool(name="const", bufs=1))
        xpool = ctx.enter_context(tc.tile_pool(name="xpool", bufs=1))
        opool = ctx.enter_context(tc.tile_pool(name="opool", bufs=1))
        gpool = ctx.enter_context(tc.tile_pool(name="gpool", bufs=3))
        cpool = ctx.enter_context(tc.tile_pool(name="cpool", bufs=4))
        tpsum = ctx.enter_context(tc.psum_pool(name="tpsum", bufs=6))
        apsum = ctx.enter_context(tc.psum_pool(name="apsum", bufs=2))

        xv = x.rearrange("(p j) k -> p (j k)", j=J)
        ov = out.rearrange("(p j) n -> p (j n)", j=J)

        zero_col = const.tile([P, 1], F32, name="zero_col")
        one_col = const.tile([P, 1], F32, name="one_col")
        warm = const.tile([P, 1], F32, name="warm")
        brow = const.tile([P, 512], BF16, name="brow")
        ones = const.tile([P, P], BF16, name="ones")
        ident = const.tile([P, P], F32, name="ident")
        nc.vector.memset(brow[:], 0.0)
        nc.vector.memset(zero_col[:], 0.0)
        nc.vector.memset(one_col[:], 1.0)
        nc.vector.memset(ones[:], 1.0)
        make_identity(nc, ident[:])
        nc.scalar.dma_start(out=brow[0:1, N : 2 * N], in_=b_std)
        nc.scalar.dma_start(out=brow[0:1, 0:N], in_=b_loc)
        nc.scalar.dma_start(out=brow[0:1, 2 * N : 3 * N], in_=eps_b)
        nc.scalar.activation(out=warm[:], in_=zero_col[:], func=ACT.Exp)

        ws = const.tile([P, K], BF16, name="ws")
        we = const.tile([P, K], BF16, name="we")
        wl = const.tile([P, K], BF16, name="wl")

        def load_w(dst, src):
            nc.sync.dma_start(
                out=dst[:].rearrange("p (b c) -> p b c", b=4),
                in_=src.rearrange("(b p e) n -> p b (e n)", b=4, p=P, e=2),
            )

        x_sb = [xpool.tile([P, CH], BF16, name="x%d" % c) for c in range(NCH)]

        load_w(ws, w_std)
        nc.sync.dma_start(out=x_sb[0][:, 0 : CH // 2], in_=xv[:, 0 : CH // 2])
        nc.sync.dma_start(out=x_sb[0][:, CH // 2 : CH], in_=xv[:, CH // 2 : CH])
        load_w(we, eps_w)
        load_w(wl, w_loc)
        for c in range(1, NCH):
            nc.sync.dma_start(out=x_sb[c][:], in_=xv[:, c * CH : (c + 1) * CH])

        banks = {}
        grouped = {}
        codes = {}
        scales = {}
        accs = {}
        otiles = {}

        def transposes(c, first, count):
            xw = x_sb[c][:].bitcast(F32)
            for jj in range(first, first + count):
                bank = tpsum.tile([P, 512], F32, name="xt")
                for b in range(4):
                    col = jj * 512 + b * P
                    nc.tensor.transpose(bank[:, b * P : (b + 1) * P], xw[:, col : col + P], ident[:])
                banks[(c, jj)] = bank

        def evacuate(c):
            g_t = gpool.tile([P, CH], BF16, name="grouped", align_bytes=64)
            grouped[c] = g_t
            gw = g_t[:].bitcast(F32)
            on_dve = dve_banks(c)
            for jj in range(JC):
                dst = gw[:, jj * 512 : (jj + 1) * 512].rearrange("p (g r u) -> p g r u", g=2, r=P, u=2)
                src = banks[(c, jj)][:].rearrange("p (g u r) -> p g r u", g=2, u=2, r=P)
                if jj in on_dve:
                    nc.vector.tensor_copy(out=dst, in_=src)
                else:
                    nc.scalar.copy(out=dst, in_=src)

        def quantise(c, part, parts):
            if part == 0:
                codes[c] = cpool.tile([P, CH // 4], U32, name="codes", align_bytes=64)
                scales[c] = cpool.tile([P, CH // 4], U8, name="scales", align_bytes=64)
            wd = CH // 4 // parts
            nc.vector.quantize_mx(
                out=codes[c][:, part * wd : (part + 1) * wd].bitcast(FP8X4),
                scales=scales[c][:, part * wd : (part + 1) * wd],
                in_=grouped[c][:, part * 4 * wd : (part + 1) * 4 * wd],
            )

        def multiply_part(c, first, count):
            if first == 0:
                acc0 = apsum.tile([P, 512], F32, name="acc")
                accs[(c, 0)] = acc0
            acc = accs[(c, 0)]
            for i in range(first, first + count):
                for g in range(2):
                    col = (i * 2 + g) * P
                    nc.tensor.matmul_mx(
                        out=acc[:, i * N : (i + 1) * N],
                        lhsT=codes[c][:, col : col + P].bitcast(FP8X4),
                        lhsT_scale=scales[c][:, col : col + P],
                        rhs=wcodes[:, g * N : (g + 1) * N].bitcast(FP8X4),
                        rhs_scale=wscales[:, g * N : (g + 1) * N],
                        start=(g == 0),
                        stop=(g == 1),
                    )

        def multiply(c, first, count, pool, name):
            acc = pool.tile([P, 512], F32, name=name)
            accs[(c, first)] = acc
            for i in range(count):
                for g in range(2):
                    col = ((first + i) * 2 + g) * P
                    nc.tensor.matmul_mx(
                        out=acc[:, i * N : (i + 1) * N],
                        lhsT=codes[c][:, col : col + P].bitcast(FP8X4),
                        lhsT_scale=scales[c][:, col : col + P],
                        rhs=wcodes[:, g * N : (g + 1) * N].bitcast(FP8X4),
                        rhs_scale=wscales[:, g * N : (g + 1) * N],
                        start=(g == 0),
                        stop=(g == 1),
                    )

        def finish(c, first, count):
            j0 = c * JC + first
            for (a, b) in STORES:
                if a <= j0 < b:
                    if a == j0:
                        otiles[a] = opool.tile([P, (b - a) * N], F32, name="o%d" % a)
                    o_t = otiles[a]
                    off = (j0 - a) * N
                    nc.vector.tensor_tensor(
                        out=o_t[:, off : off + count * N].rearrange("p (j n) -> p j n", j=count),
                        in0=accs[(c, first)][:, 0 : count * N].rearrange("p (j n) -> p j n", j=count),
                        in1=bias[:].unsqueeze(1).to_broadcast([P, count, N]),
                        op=ALU.add,
                    )
                    if j0 + count == b:
                        nc.sync.dma_start(out=ov[:, a * N : b * N], in_=o_t[:])

        na = const.tile([P, K], BF16, name="na")
        ex = const.tile([P, K + N], F32, name="ex")
        wg = const.tile([P, K], BF16, name="wg", align_bytes=64)
        wcodes = const.tile([P, K // 4], U32, name="wcodes", align_bytes=64)
        wscales = const.tile([P, K // 4], U8, name="wscales", align_bytes=64)
        bsb = const.tile([P, 3 * N], F32, name="bsb")
        nb = const.tile([P, N], F32, name="nb")
        bias = const.tile([P, N], F32, name="bias")
        eb = ex[:, K : K + N]

        bps = apsum.tile([P, 512], F32, name="acc")
        nc.tensor.matmul(out=bps[:], lhsT=ones[:], rhs=brow[:], start=True, stop=True)

        nc.vector.tensor_scalar_min(out=na[:], in0=ws[:], scalar1=CLAMP)
        nc.scalar.activation(out=ex[:, 0:K], in_=na[:], func=ACT.Exp)
        nc.vector.tensor_copy(out=bsb[:], in_=bps[:, 0 : 3 * N])
        b_l = bsb[:, 0:N]
        b_s = bsb[:, N : 2 * N]
        b_e = bsb[:, 2 * N : 3 * N]
        nc.vector.tensor_scalar_min(out=nb[:], in0=b_s, scalar1=CLAMP)
        nc.scalar.activation(out=eb, in_=nb[:], func=ACT.Exp)
        nc.scalar.activation(out=ex[:], in_=ex[:], func=ACT.Ln, bias=one_col[:], scale=1.0)

        def sample_w():
            nc.vector.tensor_tensor(out=ex[:, 0:K], in0=ex[:, 0:K], in1=ws[:], op=ALU.max)
            nc.vector.tensor_tensor(out=ex[:, 0:K], in0=ex[:, 0:K], in1=we[:], op=ALU.mult)
            nc.vector.tensor_tensor(
                out=wg[:].rearrange("p (g n t) -> p g n t", g=2, n=N, t=4),
                in0=ex[:, 0:K].rearrange("p (g t n) -> p g n t", g=2, n=N, t=4),
                in1=wl[:].rearrange("p (g t n) -> p g n t", g=2, n=N, t=4),
                op=ALU.add,
            )

        def sample_b():
            nc.vector.tensor_tensor(out=nb[:], in0=eb, in1=b_s, op=ALU.max)
            nc.vector.tensor_tensor(out=nb[:], in0=nb[:], in1=b_e, op=ALU.mult)
            nc.vector.tensor_tensor(out=bias[:], in0=nb[:], in1=b_l, op=ALU.add)

        for c in range(NCH):
            transposes(c, 0, 2)
            if c >= M_LAG:
                multiply_part(c - M_LAG, 0, 2)
            transposes(c, 2, 2)
            if c >= M_LAG:
                multiply_part(c - M_LAG, 2, 2)
            evacuate(c)
            if c >= O_LAG:
                finish(c - O_LAG, 0, JC)
            if c == 1:
                sample_w()
                sample_b()
                nc.vector.quantize_mx(out=wcodes[:].bitcast(FP8X4), scales=wscales[:], in_=wg[:])
            if c >= 1:
                quantise(c - 1, 0, 1)
        L = NCH - 1
        multiply(L - 2, 0, JC, apsum, "acc")
        finish(L - 3, 0, JC)
        quantise(L, 0, 2)
        quantise(L, 1, 2)
        multiply(L - 1, 0, JC, apsum, "acc")
        finish(L - 2, 0, JC)
        multiply(L, 0, 2, tpsum, "xt")
        multiply(L, 2, 2, tpsum, "xt")
        finish(L - 1, 0, JC)
        finish(L, 0, 2)
        finish(L, 2, 2)
